import numpy as np
import ml_dtypes

BF16 = ml_dtypes.bfloat16


def bf(x):
    return np.asarray(x, np.float32).astype(BF16)


def f32(x):
    return np.asarray(x, np.float32)


def f64(x):
    return np.asarray(x).astype(np.float64)


def striped(idx):
    return np.tile(idx.reshape(-1, 16).T, (8, 1))


D, M, S, H, K, N = 128, 256, 1024, 512, 2, 1024


def setup_inputs():
    return {"table": bf(np.random.standard_normal((D, S))), "w": bf(np.random.standard_normal((D, M)) / np.sqrt(D)), "b": f32(0.2 * np.random.standard_normal((M, 1))), "offs": striped(np.concatenate([np.random.permutation(S)[:H] for _ in range(K)]))}


def reference(table, w, b, offs):
    idx = offs[:16].T.reshape(-1)
    return np.tanh(f64(w).T @ f64(table)[:, idx] + f64(b))

@@ -1,0 +1,44 @@
+import concourse.mybir as mybir
+
+BF16, F32, U16 = mybir.dt.bfloat16, mybir.dt.float32, mybir.dt.uint16
+TANH = mybir.ActivationFunctionType.Tanh
+
+P = 128
+NODES = 1024
+N = 1024
+HALVES = 2
+PIECE = 512
+PER_COLUMN = 16
+
+FLOPS = 2 * P * HALVES * P * N
+
+
+def tile_multihead_attention_kernel(tc, table, w, b, offs, out):
+    nc = tc.nc
+    with (
+        tc.tile_pool(name="held", bufs=1) as held,
+        tc.tile_pool(name="results", bufs=4) as results,
+        tc.psum_pool(name="psum", bufs=4) as psum,
+    ):
+        offsets = held.tile([P, N // PER_COLUMN], U16, name="offsets")
+        nc.sync.dma_start(offsets[:], offs)
+        nodes = held.tile([P, NODES], BF16, name="nodes")
+        nc.sync.dma_start(nodes[:], table)
+        weights = held.tile([P, HALVES * P], BF16, name="weights")
+        nc.scalar.dma_start(weights[:], w)
+        bias = held.tile([P, HALVES], F32, name="bias")
+        with nc.allow_non_contiguous_dma(reason="256 single float32, one to a partition and half"):
+            nc.scalar.dma_start(bias[:], b.rearrange("(h p) o -> p (h o)", p=P))
+
+        for piece in range(N // PIECE):
+            columns = slice(piece * PIECE, (piece + 1) * PIECE)
+            piece_offsets = offsets[:, piece * PIECE // PER_COLUMN : (piece + 1) * PIECE // PER_COLUMN]
+            for half in range(HALVES):
+                rows = slice(half * P, (half + 1) * P)
+                projected = psum.tile([P, PIECE], F32, name="projected")
+                nc.tensor.matmul(
+                    projected[:], weights[:, rows], nodes[:].indirect(piece_offsets), start=True, stop=True
+                )
+                result = results.tile([P, PIECE], F32, name="result")
+                nc.scalar.activation(result[:], projected[:], TANH, bias=bias[:, half : half + 1])
+                nc.sync.dma_start(out[rows, columns], result[:])

@@ -30,6 +30,10 @@ def tile_multihead_attention_kernel(tc, table, w, b, offs, out):
         with nc.allow_non_contiguous_dma(reason="256 single float32, one to a partition and half"):
             nc.scalar.dma_start(bias[:], b.rearrange("(h p) o -> p (h o)", p=P))
 
+        scratch = held.tile([P, 1], F32, name="scratch")
+        nc.vector.memset(scratch[:], 0.0)
+        nc.scalar.activation(scratch[:], scratch[:], TANH)
+
         for piece in range(N // PIECE):
             columns = slice(piece * PIECE, (piece + 1) * PIECE)
             piece_offsets = offsets[:, piece * PIECE // PER_COLUMN : (piece + 1) * PIECE // PER_COLUMN]

@@ -9,6 +9,8 @@ N = 1024
 HALVES = 2
 PIECE = 512
 PER_COLUMN = 16
+WARM_UPS = 4
+WARM_UP_COLUMNS = 512
 
 FLOPS = 2 * P * HALVES * P * N
 
@@ -19,6 +21,7 @@ def tile_multihead_attention_kernel(tc, table, w, b, offs, out):
         tc.tile_pool(name="held", bufs=1) as held,
         tc.tile_pool(name="results", bufs=4) as results,
         tc.psum_pool(name="psum", bufs=4) as psum,
+        tc.psum_pool(name="unread", bufs=1) as unread,
     ):
         offsets = held.tile([P, N // PER_COLUMN], U16, name="offsets")
         nc.sync.dma_start(offsets[:], offs)
@@ -30,8 +33,14 @@ def tile_multihead_attention_kernel(tc, table, w, b, offs, out):
         with nc.allow_non_contiguous_dma(reason="256 single float32, one to a partition and half"):
             nc.scalar.dma_start(bias[:], b.rearrange("(h p) o -> p (h o)", p=P))
 
+        zeros = held.tile([P, WARM_UP_COLUMNS], BF16, name="zeros")
+        nc.vector.memset(zeros[:], 0.0)
+        ignored = unread.tile([P, WARM_UP_COLUMNS], F32, name="ignored")
+        for warm_up in range(WARM_UPS):
+            nc.tensor.matmul(ignored[:], zeros[:, 0:P], zeros[:], start=True, stop=True)
+
         scratch = held.tile([P, 1], F32, name="scratch")
-        nc.vector.memset(scratch[:], 0.0)
+        nc.gpsimd.memset(scratch[:], 0.0)
         nc.scalar.activation(scratch[:], scratch[:], TANH)
 
         for piece in range(N // PIECE):

@@ -7,10 +7,9 @@ P = 128
 NODES = 1024
 N = 1024
 HALVES = 2
-PIECE = 512
+PIECE = 256
+PRODUCTS = HALVES * N // PIECE
 PER_COLUMN = 16
-WARM_UPS = 4
-WARM_UP_COLUMNS = 512
 
 FLOPS = 2 * P * HALVES * P * N
 
@@ -19,9 +18,8 @@ def tile_multihead_attention_kernel(tc, table, w, b, offs, out):
     nc = tc.nc
     with (
         tc.tile_pool(name="held", bufs=1) as held,
-        tc.tile_pool(name="results", bufs=4) as results,
-        tc.psum_pool(name="psum", bufs=4) as psum,
-        tc.psum_pool(name="unread", bufs=1) as unread,
+        tc.tile_pool(name="results", bufs=PRODUCTS) as results,
+        tc.psum_pool(name="psum", bufs=PRODUCTS) as psum,
     ):
         offsets = held.tile([P, N // PER_COLUMN], U16, name="offsets")
         nc.sync.dma_start(offsets[:], offs)
@@ -33,14 +31,8 @@ def tile_multihead_attention_kernel(tc, table, w, b, offs, out):
         with nc.allow_non_contiguous_dma(reason="256 single float32, one to a partition and half"):
             nc.scalar.dma_start(bias[:], b.rearrange("(h p) o -> p (h o)", p=P))
 
-        zeros = held.tile([P, WARM_UP_COLUMNS], BF16, name="zeros")
-        nc.vector.memset(zeros[:], 0.0)
-        ignored = unread.tile([P, WARM_UP_COLUMNS], F32, name="ignored")
-        for warm_up in range(WARM_UPS):
-            nc.tensor.matmul(ignored[:], zeros[:, 0:P], zeros[:], start=True, stop=True)
-
         scratch = held.tile([P, 1], F32, name="scratch")
-        nc.gpsimd.memset(scratch[:], 0.0)
+        nc.vector.memset(scratch[:], 0.0)
         nc.scalar.activation(scratch[:], scratch[:], TANH)
 
         for piece in range(N // PIECE):

@@ -7,8 +7,9 @@ P = 128
 NODES = 1024
 N = 1024
 HALVES = 2
-PIECE = 256
-PRODUCTS = HALVES * N // PIECE
+PIECES = (128, 384, 384, 128)
+BANK = 512
+PRODUCTS = HALVES * len(PIECES)
 PER_COLUMN = 16
 
 FLOPS = 2 * P * HALVES * P * N
@@ -35,15 +36,17 @@ def tile_multihead_attention_kernel(tc, table, w, b, offs, out):
         nc.vector.memset(scratch[:], 0.0)
         nc.scalar.activation(scratch[:], scratch[:], TANH)
 
-        for piece in range(N // PIECE):
-            columns = slice(piece * PIECE, (piece + 1) * PIECE)
-            piece_offsets = offsets[:, piece * PIECE // PER_COLUMN : (piece + 1) * PIECE // PER_COLUMN]
+        first = 0
+        for length in PIECES:
+            columns = slice(first, first + length)
+            piece_offsets = offsets[:, first // PER_COLUMN : (first + length) // PER_COLUMN]
             for half in range(HALVES):
                 rows = slice(half * P, (half + 1) * P)
-                projected = psum.tile([P, PIECE], F32, name="projected")
+                projected = psum.tile([P, BANK], F32, name="projected")
                 nc.tensor.matmul(
-                    projected[:], weights[:, rows], nodes[:].indirect(piece_offsets), start=True, stop=True
+                    projected[:, :length], weights[:, rows], nodes[:].indirect(piece_offsets), start=True, stop=True
                 )
-                result = results.tile([P, PIECE], F32, name="result")
-                nc.scalar.activation(result[:], projected[:], TANH, bias=bias[:, half : half + 1])
-                nc.sync.dma_start(out[rows, columns], result[:])
+                result = results.tile([P, BANK], F32, name="result")
+                nc.scalar.activation(result[:, :length], projected[:, :length], TANH, bias=bias[:, half : half + 1])
+                nc.sync.dma_start(out[rows, columns], result[:, :length])
+            first += length

@@ -7,7 +7,7 @@ P = 128
 NODES = 1024
 N = 1024
 HALVES = 2
-PIECES = (128, 384, 384, 128)
+PIECES = (160, 224, 288, 352)
 BANK = 512
 PRODUCTS = HALVES * len(PIECES)
 PER_COLUMN = 16

@@ -28,9 +28,12 @@ def tile_multihead_attention_kernel(tc, table, w, b, offs, out):
         nc.sync.dma_start(nodes[:], table)
         weights = held.tile([P, HALVES * P], BF16, name="weights")
         nc.scalar.dma_start(weights[:], w)
-        bias = held.tile([P, HALVES], F32, name="bias")
-        with nc.allow_non_contiguous_dma(reason="256 single float32, one to a partition and half"):
-            nc.scalar.dma_start(bias[:], b.rearrange("(h p) o -> p (h o)", p=P))
+        biases = []
+        for half in range(HALVES):
+            half_bias = held.tile([P, 1], F32, name="bias%d" % half)
+            with nc.allow_non_contiguous_dma(reason="128 single float32, one to a partition"):
+                nc.scalar.dma_start(half_bias[:], b[half * P : (half + 1) * P, :])
+            biases.append(half_bias)
 
         scratch = held.tile([P, 1], F32, name="scratch")
         nc.vector.memset(scratch[:], 0.0)
@@ -47,6 +50,6 @@ def tile_multihead_attention_kernel(tc, table, w, b, offs, out):
                     projected[:, :length], weights[:, rows], nodes[:].indirect(piece_offsets), start=True, stop=True
                 )
                 result = results.tile([P, BANK], F32, name="result")
-                nc.scalar.activation(result[:, :length], projected[:, :length], TANH, bias=bias[:, half : half + 1])
+                nc.scalar.activation(result[:, :length], projected[:, :length], TANH, bias=biases[half][:])
                 nc.sync.dma_start(out[rows, columns], result[:, :length])
             first += length

@@ -26,14 +26,11 @@ def tile_multihead_attention_kernel(tc, table, w, b, offs, out):
         nc.sync.dma_start(offsets[:], offs)
         nodes = held.tile([P, NODES], BF16, name="nodes")
         nc.sync.dma_start(nodes[:], table)
+        biases = held.tile([P, HALVES], F32, name="biases")
+        nc.scalar.dma_start(biases[:], b.rearrange("(p h) o -> p (h o)", h=HALVES))
         weights = held.tile([P, HALVES * P], BF16, name="weights")
         nc.scalar.dma_start(weights[:], w)
-        biases = []
-        for half in range(HALVES):
-            half_bias = held.tile([P, 1], F32, name="bias%d" % half)
-            with nc.allow_non_contiguous_dma(reason="128 single float32, one to a partition"):
-                nc.scalar.dma_start(half_bias[:], b[half * P : (half + 1) * P, :])
-            biases.append(half_bias)
+        out_rows = out.rearrange("(p h) n -> h p n", h=HALVES)
 
         scratch = held.tile([P, 1], F32, name="scratch")
         nc.vector.memset(scratch[:], 0.0)
@@ -44,12 +41,11 @@ def tile_multihead_attention_kernel(tc, table, w, b, offs, out):
             columns = slice(first, first + length)
             piece_offsets = offsets[:, first // PER_COLUMN : (first + length) // PER_COLUMN]
             for half in range(HALVES):
-                rows = slice(half * P, (half + 1) * P)
                 projected = psum.tile([P, BANK], F32, name="projected")
                 nc.tensor.matmul(
-                    projected[:, :length], weights[:, rows], nodes[:].indirect(piece_offsets), start=True, stop=True
+                    projected[:, :length], weights[:, half::HALVES], nodes[:].indirect(piece_offsets), start=True, stop=True
                 )
                 result = results.tile([P, BANK], F32, name="result")
-                nc.scalar.activation(result[:, :length], projected[:, :length], TANH, bias=biases[half][:])
-                nc.sync.dma_start(out[rows, columns], result[:, :length])
+                nc.scalar.activation(result[:, :length], projected[:, :length], TANH, bias=biases[:, half : half + 1])
+                nc.sync.dma_start(out_rows[half, :, columns], result[:, :length])
             first += length

@@ -26,10 +26,10 @@ def tile_multihead_attention_kernel(tc, table, w, b, offs, out):
         nc.sync.dma_start(offsets[:], offs)
         nodes = held.tile([P, NODES], BF16, name="nodes")
         nc.sync.dma_start(nodes[:], table)
-        biases = held.tile([P, HALVES], F32, name="biases")
-        nc.scalar.dma_start(biases[:], b.rearrange("(p h) o -> p (h o)", h=HALVES))
         weights = held.tile([P, HALVES * P], BF16, name="weights")
         nc.scalar.dma_start(weights[:], w)
+        biases = held.tile([P, HALVES], F32, name="biases")
+        nc.scalar.dma_start(biases[:], b.rearrange("(p h) o -> p (h o)", h=HALVES))
         out_rows = out.rearrange("(p h) n -> h p n", h=HALVES)
 
         scratch = held.tile([P, 1], F32, name="scratch")

@@ -22,10 +22,10 @@ def tile_multihead_attention_kernel(tc, table, w, b, offs, out):
         tc.tile_pool(name="results", bufs=PRODUCTS) as results,
         tc.psum_pool(name="psum", bufs=PRODUCTS) as psum,
     ):
-        offsets = held.tile([P, N // PER_COLUMN], U16, name="offsets")
-        nc.sync.dma_start(offsets[:], offs)
         nodes = held.tile([P, NODES], BF16, name="nodes")
         nc.sync.dma_start(nodes[:], table)
+        offsets = held.tile([P, N // PER_COLUMN], U16, name="offsets")
+        nc.sync.dma_start(offsets[:], offs)
         weights = held.tile([P, HALVES * P], BF16, name="weights")
         nc.scalar.dma_start(weights[:], w)
         biases = held.tile([P, HALVES], F32, name="biases")

import concourse.mybir as mybir

BF16, F32, U16 = mybir.dt.bfloat16, mybir.dt.float32, mybir.dt.uint16
TANH = mybir.ActivationFunctionType.Tanh

P = 128
NODES = 1024
N = 1024
HALVES = 2
PIECES = (160, 224, 288, 352)
BANK = 512
PRODUCTS = HALVES * len(PIECES)
PER_COLUMN = 16

FLOPS = 2 * P * HALVES * P * N


def tile_multihead_attention_kernel(tc, table, w, b, offs, out):
    nc = tc.nc
    with (
        tc.tile_pool(name="held", bufs=1) as held,
        tc.tile_pool(name="results", bufs=PRODUCTS) as results,
        tc.psum_pool(name="psum", bufs=PRODUCTS) as psum,
    ):
        nodes = held.tile([P, NODES], BF16, name="nodes")
        nc.sync.dma_start(nodes[:], table)
        offsets = held.tile([P, N // PER_COLUMN], U16, name="offsets")
        nc.sync.dma_start(offsets[:], offs)
        weights = held.tile([P, HALVES * P], BF16, name="weights")
        nc.scalar.dma_start(weights[:], w)
        biases = held.tile([P, HALVES], F32, name="biases")
        nc.scalar.dma_start(biases[:], b.rearrange("(p h) o -> p (h o)", h=HALVES))
        out_rows = out.rearrange("(p h) n -> h p n", h=HALVES)

        scratch = held.tile([P, 1], F32, name="scratch")
        nc.vector.memset(scratch[:], 0.0)
        nc.scalar.activation(scratch[:], scratch[:], TANH)

        first = 0
        for length in PIECES:
            columns = slice(first, first + length)
            piece_offsets = offsets[:, first // PER_COLUMN : (first + length) // PER_COLUMN]
            for half in range(HALVES):
                projected = psum.tile([P, BANK], F32, name="projected")
                nc.tensor.matmul(
                    projected[:, :length], weights[:, half::HALVES], nodes[:].indirect(piece_offsets), start=True, stop=True
                )
                result = results.tile([P, BANK], F32, name="result")
                nc.scalar.activation(result[:, :length], projected[:, :length], TANH, bias=biases[:, half : half + 1])
                nc.sync.dma_start(out_rows[half, :, columns], result[:, :length])
            first += length
